import numpy as np
import ml_dtypes

BF16 = ml_dtypes.bfloat16


def bf(x):
    return np.asarray(x, np.float32).astype(BF16)


def f32(x):
    return np.asarray(x, np.float32)


def f64(x):
    return np.asarray(x).astype(np.float64)


def striped(idx):
    return np.tile(idx.reshape(-1, 16).T, (8, 1))


S, D, F, N = 256, 128, 512, 128
EPS = 1e-5


def gelu_tanh(v):
    return 0.5 * v * (1.0 + np.tanh(np.sqrt(2.0 / np.pi) * (v + 0.044715 * v**3)))


def setup_inputs():
    return {
        "table": bf(np.random.standard_normal((S, D))),
        "act": f32(0.5 * np.random.standard_normal((D, 1))),
        "lnw": f32(1.0 + 0.1 * np.random.standard_normal((D, 1))),
        "lnb": f32(0.1 * np.random.standard_normal((D, 1))),
        "w1": bf(np.random.standard_normal((D, F)) / np.sqrt(D)),
        "b1": f32(0.1 * np.random.standard_normal((F, 1))),
        "w2": bf(np.random.standard_normal((F, D)) / np.sqrt(F)),
        "b2": f32(0.1 * np.random.standard_normal((D, 1))),
        "offs": striped(np.random.permutation(S)[:N]),
    }


def reference(table, act, lnw, lnb, w1, b1, w2, b2, offs):
    idx = offs[:16].T.reshape(-1)
    x = f64(table).T + f64(act)
    mean = x.mean(axis=0, keepdims=True)
    var = ((x - mean) ** 2).mean(axis=0, keepdims=True)
    n = (x - mean) / np.sqrt(var + EPS) * f64(lnw) + f64(lnb)
    h = gelu_tanh(f64(w1).T @ n[:, idx] + f64(b1))
    return x[:, idx] + f64(w2).T @ h + f64(b2)

@@ -1,0 +1,108 @@
+import concourse.mybir as mybir
+from concourse.masks import make_identity
+
+S, D, F, N = 256, 128, 512, 128
+P = 128
+EPS = 1e-5
+WORD_BLOCKS = S // P
+HIDDEN_BLOCKS = F // P
+FLOPS = 2 * N * D * F * 2
+
+BF16, F32, U16 = mybir.dt.bfloat16, mybir.dt.float32, mybir.dt.uint16
+ALU = mybir.AluOpType
+FUNC = mybir.ActivationFunctionType
+
+
+def tile_biojepa_kernel(tc, table, act, lnw, lnb, w1, b1, w2, b2, offs, out):
+    nc = tc.nc
+    with (
+        tc.tile_pool(name="held", bufs=1) as held,
+        tc.psum_pool(name="psum", bufs=1) as psum,
+    ):
+        table_rows = held.tile([P, WORD_BLOCKS, D], BF16)
+        nc.sync.dma_start(table_rows[:], table.rearrange("(b p) d -> p b d", p=P))
+        act_rows = held.tile([P, D], F32)
+        nc.scalar.dma_start(act_rows[:], act.rearrange("d o -> (d o)").partition_broadcast(P))
+        offsets = held.tile([P, N // 16], U16)
+        nc.sync.dma_start(offsets[:], offs)
+
+        lnw_col = held.tile([P, 1], F32)
+        nc.scalar.dma_start(lnw_col[:], lnw)
+        lnb_col = held.tile([P, 1], F32)
+        nc.scalar.dma_start(lnb_col[:], lnb)
+        w1_sb = held.tile([P, F], BF16)
+        nc.sync.dma_start(w1_sb[:], w1)
+        b1_cols = held.tile([P, HIDDEN_BLOCKS], F32)
+        with nc.allow_non_contiguous_dma(reason="512 biases, one to a partition and block"):
+            nc.scalar.dma_start(b1_cols[:], b1.rearrange("(k p) o -> p (k o)", p=P))
+        w2_sb = held.tile([P, HIDDEN_BLOCKS, D], BF16)
+        nc.sync.dma_start(w2_sb[:], w2.rearrange("(k p) d -> p k d", p=P))
+        act_col = held.tile([P, 1], F32)
+        nc.gpsimd.dma_start(act_col[:], act)
+        b2_col = held.tile([P, 1], F32)
+        nc.gpsimd.dma_start(b2_col[:], b2)
+
+        identity_f32 = held.tile([P, P], F32)
+        make_identity(nc, identity_f32[:])
+        identity_bf16 = held.tile([P, P], BF16)
+        make_identity(nc, identity_bf16[:])
+        eps_col = held.tile([P, 1], F32)
+        nc.vector.memset(eps_col[:], EPS)
+
+        x = held.tile([P, WORD_BLOCKS, D], F32)
+        stats = held.tile([P, WORD_BLOCKS, 6], F32)
+        mean_var = held.tile([P, WORD_BLOCKS, 2], F32)
+        for b in range(WORD_BLOCKS):
+            nc.vector.tensor_tensor(x[:, b, :], table_rows[:, b, :], act_rows[:], ALU.add)
+        for b in range(WORD_BLOCKS):
+            nc.vector.bn_stats(stats[:, b, :], x[:, b, :])
+        for b in range(WORD_BLOCKS):
+            nc.vector.bn_aggr(mean_var[:, b, :], stats[:, b, :])
+        std = held.tile([P, WORD_BLOCKS], F32)
+        nc.scalar.activation(std[:], mean_var[:, :, 1], FUNC.Sqrt, bias=eps_col[:], scale=1.0)
+        rstd = held.tile([P, WORD_BLOCKS], F32)
+        nc.vector.reciprocal(rstd[:], std[:])
+        z = held.tile([P, WORD_BLOCKS, D], F32)
+        for b in range(WORD_BLOCKS):
+            nc.vector.tensor_scalar(
+                z[:, b, :], x[:, b, :], mean_var[:, b, 0:1], rstd[:, b : b + 1], ALU.subtract, ALU.mult
+            )
+
+        z_flipped = psum.tile([P, S], F32)
+        for b in range(WORD_BLOCKS):
+            nc.tensor.transpose(z_flipped[:, b * P : (b + 1) * P], z[:, b, :], identity_f32[:])
+        n_window = held.tile([P, S], BF16)
+        nc.vector.tensor_scalar(n_window[:], z_flipped[:], lnw_col[:], lnb_col[:], ALU.mult, ALU.add)
+
+        table_flipped = psum.tile([P, S], BF16)
+        for b in range(WORD_BLOCKS):
+            nc.tensor.transpose(table_flipped[:, b * P : (b + 1) * P], table_rows[:, b, :], identity_bf16[:])
+        table_window = held.tile([P, S], BF16)
+        nc.vector.tensor_copy(table_window[:], table_flipped[:])
+
+        hidden_psum = [psum.tile([P, N], F32, name=f"hidden_psum{k}") for k in range(HIDDEN_BLOCKS)]
+        for k in range(HIDDEN_BLOCKS):
+            nc.tensor.matmul(
+                hidden_psum[k][:],
+                w1_sb[:, k * P : (k + 1) * P],
+                n_window[:].indirect(offsets[:]),
+                start=True,
+                stop=True,
+            )
+        out_psum = psum.tile([P, N], F32)
+        nc.tensor.matmul(
+            out_psum[:], identity_bf16[:], table_window[:].indirect(offsets[:]), start=True, stop=False
+        )
+
+        h = held.tile([P, HIDDEN_BLOCKS, N], BF16)
+        for k in range(HIDDEN_BLOCKS):
+            nc.scalar.activation(
+                h[:, k, :], hidden_psum[k][:], FUNC.Gelu_apprx_tanh, bias=b1_cols[:, k : k + 1], scale=1.0
+            )
+            nc.tensor.matmul(
+                out_psum[:], w2_sb[:, k, :], h[:, k, :], start=False, stop=(k == HIDDEN_BLOCKS - 1)
+            )
+
+        out_sb = held.tile([P, N], F32)
+        nc.vector.tensor_scalar(out_sb[:], out_psum[:], act_col[:], b2_col[:], ALU.add, ALU.add)
+        nc.sync.dma_start(out, out_sb[:])

@@ -38,16 +38,21 @@ def tile_biojepa_kernel(tc, table, act, lnw, lnb, w1, b1, w2, b2, offs, out):
         w2_sb = held.tile([P, HIDDEN_BLOCKS, D], BF16)
         nc.sync.dma_start(w2_sb[:], w2.rearrange("(k p) d -> p k d", p=P))
         act_col = held.tile([P, 1], F32)
-        nc.gpsimd.dma_start(act_col[:], act)
+        nc.scalar.dma_start(act_col[:], act)
         b2_col = held.tile([P, 1], F32)
-        nc.gpsimd.dma_start(b2_col[:], b2)
+        nc.sync.dma_start(b2_col[:], b2)
 
-        identity_f32 = held.tile([P, P], F32)
-        make_identity(nc, identity_f32[:])
         identity_bf16 = held.tile([P, P], BF16)
         make_identity(nc, identity_bf16[:])
+        identity_f32 = held.tile([P, P], F32)
+        make_identity(nc, identity_f32[:])
         eps_col = held.tile([P, 1], F32)
         nc.vector.memset(eps_col[:], EPS)
+
+        table_flipped = psum.tile([P, S], BF16)
+        for b in range(WORD_BLOCKS):
+            nc.tensor.transpose(table_flipped[:, b * P : (b + 1) * P], table_rows[:, b, :], identity_bf16[:])
+        table_window = held.tile([P, S], BF16)
 
         x = held.tile([P, WORD_BLOCKS, D], F32)
         stats = held.tile([P, WORD_BLOCKS, 6], F32)
@@ -60,6 +65,7 @@ def tile_biojepa_kernel(tc, table, act, lnw, lnb, w1, b1, w2, b2, offs, out):
             nc.vector.bn_aggr(mean_var[:, b, :], stats[:, b, :])
         std = held.tile([P, WORD_BLOCKS], F32)
         nc.scalar.activation(std[:], mean_var[:, :, 1], FUNC.Sqrt, bias=eps_col[:], scale=1.0)
+        nc.vector.tensor_copy(table_window[:], table_flipped[:])
         rstd = held.tile([P, WORD_BLOCKS], F32)
         nc.vector.reciprocal(rstd[:], std[:])
         z = held.tile([P, WORD_BLOCKS, D], F32)
@@ -68,18 +74,19 @@ def tile_biojepa_kernel(tc, table, act, lnw, lnb, w1, b1, w2, b2, offs, out):
                 z[:, b, :], x[:, b, :], mean_var[:, b, 0:1], rstd[:, b : b + 1], ALU.subtract, ALU.mult
             )
 
-        z_flipped = psum.tile([P, S], F32)
-        for b in range(WORD_BLOCKS):
-            nc.tensor.transpose(z_flipped[:, b * P : (b + 1) * P], z[:, b, :], identity_f32[:])
         n_window = held.tile([P, S], BF16)
-        nc.vector.tensor_scalar(n_window[:], z_flipped[:], lnw_col[:], lnb_col[:], ALU.mult, ALU.add)
-
-        table_flipped = psum.tile([P, S], BF16)
+        z_flipped = [psum.tile([P, P], F32, name=f"z_flipped{b}") for b in range(WORD_BLOCKS)]
         for b in range(WORD_BLOCKS):
-            nc.tensor.transpose(table_flipped[:, b * P : (b + 1) * P], table_rows[:, b, :], identity_bf16[:])
-        table_window = held.tile([P, S], BF16)
-        nc.vector.tensor_copy(table_window[:], table_flipped[:])
+            nc.tensor.transpose(z_flipped[b][:], z[:, b, :], identity_f32[:])
+        for b in range(WORD_BLOCKS):
+            nc.vector.tensor_scalar(
+                n_window[:, b * P : (b + 1) * P], z_flipped[b][:], lnw_col[:], lnb_col[:], ALU.mult, ALU.add
+            )
 
+        out_psum = psum.tile([P, N], F32)
+        nc.tensor.matmul(
+            out_psum[:], identity_bf16[:], table_window[:].indirect(offsets[:]), start=True, stop=False
+        )
         hidden_psum = [psum.tile([P, N], F32, name=f"hidden_psum{k}") for k in range(HIDDEN_BLOCKS)]
         for k in range(HIDDEN_BLOCKS):
             nc.tensor.matmul(
@@ -89,10 +96,6 @@ def tile_biojepa_kernel(tc, table, act, lnw, lnb, w1, b1, w2, b2, offs, out):
                 start=True,
                 stop=True,
             )
-        out_psum = psum.tile([P, N], F32)
-        nc.tensor.matmul(
-            out_psum[:], identity_bf16[:], table_window[:].indirect(offsets[:]), start=True, stop=False
-        )
 
         h = held.tile([P, HIDDEN_BLOCKS, N], BF16)
         for k in range(HIDDEN_BLOCKS):

@@ -25,20 +25,19 @@ def tile_biojepa_kernel(tc, table, act, lnw, lnb, w1, b1, w2, b2, offs, out):
         nc.scalar.dma_start(act_rows[:], act.rearrange("d o -> (d o)").partition_broadcast(P))
         offsets = held.tile([P, N // 16], U16)
         nc.sync.dma_start(offsets[:], offs)
-
         lnw_col = held.tile([P, 1], F32)
-        nc.scalar.dma_start(lnw_col[:], lnw)
+        nc.sync.dma_start(lnw_col[:], lnw)
         lnb_col = held.tile([P, 1], F32)
-        nc.scalar.dma_start(lnb_col[:], lnb)
+        nc.sync.dma_start(lnb_col[:], lnb)
         w1_sb = held.tile([P, F], BF16)
         nc.sync.dma_start(w1_sb[:], w1)
         b1_cols = held.tile([P, HIDDEN_BLOCKS], F32)
         with nc.allow_non_contiguous_dma(reason="512 biases, one to a partition and block"):
-            nc.scalar.dma_start(b1_cols[:], b1.rearrange("(k p) o -> p (k o)", p=P))
+            nc.sync.dma_start(b1_cols[:], b1.rearrange("(k p) o -> p (k o)", p=P))
         w2_sb = held.tile([P, HIDDEN_BLOCKS, D], BF16)
         nc.sync.dma_start(w2_sb[:], w2.rearrange("(k p) d -> p k d", p=P))
         act_col = held.tile([P, 1], F32)
-        nc.scalar.dma_start(act_col[:], act)
+        nc.sync.dma_start(act_col[:], act)
         b2_col = held.tile([P, 1], F32)
         nc.sync.dma_start(b2_col[:], b2)
 

@@ -23,12 +23,12 @@ def tile_biojepa_kernel(tc, table, act, lnw, lnb, w1, b1, w2, b2, offs, out):
         nc.sync.dma_start(table_rows[:], table.rearrange("(b p) d -> p b d", p=P))
         act_rows = held.tile([P, D], F32)
         nc.scalar.dma_start(act_rows[:], act.rearrange("d o -> (d o)").partition_broadcast(P))
+        lnw_rows = held.tile([P, D], F32)
+        nc.sync.dma_start(lnw_rows[:], lnw.rearrange("d o -> (d o)").partition_broadcast(P))
+        lnb_rows = held.tile([P, D], F32)
+        nc.sync.dma_start(lnb_rows[:], lnb.rearrange("d o -> (d o)").partition_broadcast(P))
         offsets = held.tile([P, N // 16], U16)
         nc.sync.dma_start(offsets[:], offs)
-        lnw_col = held.tile([P, 1], F32)
-        nc.sync.dma_start(lnw_col[:], lnw)
-        lnb_col = held.tile([P, 1], F32)
-        nc.sync.dma_start(lnb_col[:], lnb)
         w1_sb = held.tile([P, F], BF16)
         nc.sync.dma_start(w1_sb[:], w1)
         b1_cols = held.tile([P, HIDDEN_BLOCKS], F32)
@@ -43,8 +43,6 @@ def tile_biojepa_kernel(tc, table, act, lnw, lnb, w1, b1, w2, b2, offs, out):
 
         identity_bf16 = held.tile([P, P], BF16)
         make_identity(nc, identity_bf16[:])
-        identity_f32 = held.tile([P, P], F32)
-        make_identity(nc, identity_f32[:])
         eps_col = held.tile([P, 1], F32)
         nc.vector.memset(eps_col[:], EPS)
 
@@ -64,23 +62,26 @@ def tile_biojepa_kernel(tc, table, act, lnw, lnb, w1, b1, w2, b2, offs, out):
             nc.vector.bn_aggr(mean_var[:, b, :], stats[:, b, :])
         std = held.tile([P, WORD_BLOCKS], F32)
         nc.scalar.activation(std[:], mean_var[:, :, 1], FUNC.Sqrt, bias=eps_col[:], scale=1.0)
-        nc.vector.tensor_copy(table_window[:], table_flipped[:])
+        centred = held.tile([P, WORD_BLOCKS, D], F32)
+        for b in range(WORD_BLOCKS):
+            nc.vector.scalar_tensor_tensor(
+                centred[:, b, :], x[:, b, :], mean_var[:, b, 0:1], lnw_rows[:], ALU.subtract, ALU.mult
+            )
         rstd = held.tile([P, WORD_BLOCKS], F32)
         nc.vector.reciprocal(rstd[:], std[:])
-        z = held.tile([P, WORD_BLOCKS, D], F32)
+        n_rows = held.tile([P, WORD_BLOCKS, D], BF16)
         for b in range(WORD_BLOCKS):
-            nc.vector.tensor_scalar(
-                z[:, b, :], x[:, b, :], mean_var[:, b, 0:1], rstd[:, b : b + 1], ALU.subtract, ALU.mult
+            nc.vector.scalar_tensor_tensor(
+                n_rows[:, b, :], centred[:, b, :], rstd[:, b : b + 1], lnb_rows[:], ALU.mult, ALU.add
             )
 
+        n_flipped = [psum.tile([P, P], BF16, name=f"n_flipped{b}") for b in range(WORD_BLOCKS)]
+        for b in range(WORD_BLOCKS):
+            nc.tensor.transpose(n_flipped[b][:], n_rows[:, b, :], identity_bf16[:])
+        nc.vector.tensor_copy(table_window[:], table_flipped[:])
         n_window = held.tile([P, S], BF16)
-        z_flipped = [psum.tile([P, P], F32, name=f"z_flipped{b}") for b in range(WORD_BLOCKS)]
         for b in range(WORD_BLOCKS):
-            nc.tensor.transpose(z_flipped[b][:], z[:, b, :], identity_f32[:])
-        for b in range(WORD_BLOCKS):
-            nc.vector.tensor_scalar(
-                n_window[:, b * P : (b + 1) * P], z_flipped[b][:], lnw_col[:], lnb_col[:], ALU.mult, ALU.add
-            )
+            nc.vector.tensor_copy(n_window[:, b * P : (b + 1) * P], n_flipped[b][:])
 
         out_psum = psum.tile([P, N], F32)
         nc.tensor.matmul(

@@ -43,8 +43,8 @@ def tile_biojepa_kernel(tc, table, act, lnw, lnb, w1, b1, w2, b2, offs, out):
 
         identity_bf16 = held.tile([P, P], BF16)
         make_identity(nc, identity_bf16[:])
-        eps_col = held.tile([P, 1], F32)
-        nc.vector.memset(eps_col[:], EPS)
+        minus_half = held.tile([P, WORD_BLOCKS], F32)
+        nc.vector.memset(minus_half[:], -0.5)
 
         table_flipped = psum.tile([P, S], BF16)
         for b in range(WORD_BLOCKS):
@@ -60,15 +60,15 @@ def tile_biojepa_kernel(tc, table, act, lnw, lnb, w1, b1, w2, b2, offs, out):
             nc.vector.bn_stats(stats[:, b, :], x[:, b, :])
         for b in range(WORD_BLOCKS):
             nc.vector.bn_aggr(mean_var[:, b, :], stats[:, b, :])
-        std = held.tile([P, WORD_BLOCKS], F32)
-        nc.scalar.activation(std[:], mean_var[:, :, 1], FUNC.Sqrt, bias=eps_col[:], scale=1.0)
+        var_eps = held.tile([P, WORD_BLOCKS], F32)
+        nc.vector.tensor_scalar_add(var_eps[:], mean_var[:, :, 1], EPS)
+        rstd = held.tile([P, WORD_BLOCKS], F32)
+        nc.gpsimd.tensor_tensor(rstd[:], var_eps[:], minus_half[:], ALU.pow)
         centred = held.tile([P, WORD_BLOCKS, D], F32)
         for b in range(WORD_BLOCKS):
             nc.vector.scalar_tensor_tensor(
                 centred[:, b, :], x[:, b, :], mean_var[:, b, 0:1], lnw_rows[:], ALU.subtract, ALU.mult
             )
-        rstd = held.tile([P, WORD_BLOCKS], F32)
-        nc.vector.reciprocal(rstd[:], std[:])
         n_rows = held.tile([P, WORD_BLOCKS, D], BF16)
         for b in range(WORD_BLOCKS):
             nc.vector.scalar_tensor_tensor(

@@ -7,6 +7,8 @@ EPS = 1e-5
 WORD_BLOCKS = S // P
 HIDDEN_BLOCKS = F // P
 FLOPS = 2 * N * D * F * 2
+BANK = 512
+WARM_UP = 4
 
 BF16, F32, U16 = mybir.dt.bfloat16, mybir.dt.float32, mybir.dt.uint16
 ALU = mybir.AluOpType
@@ -43,13 +45,21 @@ def tile_biojepa_kernel(tc, table, act, lnw, lnb, w1, b1, w2, b2, offs, out):
 
         identity_bf16 = held.tile([P, P], BF16)
         make_identity(nc, identity_bf16[:])
-        minus_half = held.tile([P, WORD_BLOCKS], F32)
-        nc.vector.memset(minus_half[:], -0.5)
+        eps_col = held.tile([P, 1], F32)
+        nc.vector.memset(eps_col[:], EPS)
+
+        zeros = held.tile([P, BANK], BF16)
+        nc.vector.memset(zeros[:], 0.0)
+        idle_psum = psum.tile([P, BANK], F32, tag="hidden_psum3")
+        for i in range(WARM_UP):
+            nc.tensor.matmul(idle_psum[:], zeros[:, 0:P], zeros[:], start=True, stop=True)
 
         table_flipped = psum.tile([P, S], BF16)
         for b in range(WORD_BLOCKS):
             nc.tensor.transpose(table_flipped[:, b * P : (b + 1) * P], table_rows[:, b, :], identity_bf16[:])
         table_window = held.tile([P, S], BF16)
+        for i in range(WARM_UP):
+            nc.tensor.matmul(idle_psum[:], zeros[:, 0:P], zeros[:], start=True, stop=True)
 
         x = held.tile([P, WORD_BLOCKS, D], F32)
         stats = held.tile([P, WORD_BLOCKS, 6], F32)
@@ -60,15 +70,15 @@ def tile_biojepa_kernel(tc, table, act, lnw, lnb, w1, b1, w2, b2, offs, out):
             nc.vector.bn_stats(stats[:, b, :], x[:, b, :])
         for b in range(WORD_BLOCKS):
             nc.vector.bn_aggr(mean_var[:, b, :], stats[:, b, :])
-        var_eps = held.tile([P, WORD_BLOCKS], F32)
-        nc.vector.tensor_scalar_add(var_eps[:], mean_var[:, :, 1], EPS)
-        rstd = held.tile([P, WORD_BLOCKS], F32)
-        nc.gpsimd.tensor_tensor(rstd[:], var_eps[:], minus_half[:], ALU.pow)
+        std = held.tile([P, WORD_BLOCKS], F32)
+        nc.scalar.activation(std[:], mean_var[:, :, 1], FUNC.Sqrt, bias=eps_col[:], scale=1.0)
         centred = held.tile([P, WORD_BLOCKS, D], F32)
         for b in range(WORD_BLOCKS):
             nc.vector.scalar_tensor_tensor(
                 centred[:, b, :], x[:, b, :], mean_var[:, b, 0:1], lnw_rows[:], ALU.subtract, ALU.mult
             )
+        rstd = held.tile([P, WORD_BLOCKS], F32)
+        nc.vector.reciprocal(rstd[:], std[:])
         n_rows = held.tile([P, WORD_BLOCKS, D], BF16)
         for b in range(WORD_BLOCKS):
             nc.vector.scalar_tensor_tensor(

@@ -7,8 +7,6 @@ EPS = 1e-5
 WORD_BLOCKS = S // P
 HIDDEN_BLOCKS = F // P
 FLOPS = 2 * N * D * F * 2
-BANK = 512
-WARM_UP = 4
 
 BF16, F32, U16 = mybir.dt.bfloat16, mybir.dt.float32, mybir.dt.uint16
 ALU = mybir.AluOpType
@@ -25,6 +23,9 @@ def tile_biojepa_kernel(tc, table, act, lnw, lnb, w1, b1, w2, b2, offs, out):
         nc.sync.dma_start(table_rows[:], table.rearrange("(b p) d -> p b d", p=P))
         act_rows = held.tile([P, D], F32)
         nc.scalar.dma_start(act_rows[:], act.rearrange("d o -> (d o)").partition_broadcast(P))
+        b1_cols = held.tile([P, HIDDEN_BLOCKS], F32)
+        with nc.allow_non_contiguous_dma(reason="512 biases, one to a partition and block"):
+            nc.scalar.dma_start(b1_cols[:], b1.rearrange("(k p) o -> p (k o)", p=P))
         lnw_rows = held.tile([P, D], F32)
         nc.sync.dma_start(lnw_rows[:], lnw.rearrange("d o -> (d o)").partition_broadcast(P))
         lnb_rows = held.tile([P, D], F32)
@@ -33,9 +34,6 @@ def tile_biojepa_kernel(tc, table, act, lnw, lnb, w1, b1, w2, b2, offs, out):
         nc.sync.dma_start(offsets[:], offs)
         w1_sb = held.tile([P, F], BF16)
         nc.sync.dma_start(w1_sb[:], w1)
-        b1_cols = held.tile([P, HIDDEN_BLOCKS], F32)
-        with nc.allow_non_contiguous_dma(reason="512 biases, one to a partition and block"):
-            nc.sync.dma_start(b1_cols[:], b1.rearrange("(k p) o -> p (k o)", p=P))
         w2_sb = held.tile([P, HIDDEN_BLOCKS, D], BF16)
         nc.sync.dma_start(w2_sb[:], w2.rearrange("(k p) d -> p k d", p=P))
         act_col = held.tile([P, 1], F32)
@@ -48,18 +46,10 @@ def tile_biojepa_kernel(tc, table, act, lnw, lnb, w1, b1, w2, b2, offs, out):
         eps_col = held.tile([P, 1], F32)
         nc.vector.memset(eps_col[:], EPS)
 
-        zeros = held.tile([P, BANK], BF16)
-        nc.vector.memset(zeros[:], 0.0)
-        idle_psum = psum.tile([P, BANK], F32, tag="hidden_psum3")
-        for i in range(WARM_UP):
-            nc.tensor.matmul(idle_psum[:], zeros[:, 0:P], zeros[:], start=True, stop=True)
-
         table_flipped = psum.tile([P, S], BF16)
         for b in range(WORD_BLOCKS):
             nc.tensor.transpose(table_flipped[:, b * P : (b + 1) * P], table_rows[:, b, :], identity_bf16[:])
         table_window = held.tile([P, S], BF16)
-        for i in range(WARM_UP):
-            nc.tensor.matmul(idle_psum[:], zeros[:, 0:P], zeros[:], start=True, stop=True)
 
         x = held.tile([P, WORD_BLOCKS, D], F32)
         stats = held.tile([P, WORD_BLOCKS, 6], F32)

@@ -8,6 +8,9 @@ WORD_BLOCKS = S // P
 HIDDEN_BLOCKS = F // P
 FLOPS = 2 * N * D * F * 2
 
+LNW, LNB, ACT, B2, B1 = 0, 1, 2, 3, 4
+SMALL_VECTORS = B1 + HIDDEN_BLOCKS
+
 BF16, F32, U16 = mybir.dt.bfloat16, mybir.dt.float32, mybir.dt.uint16
 ALU = mybir.AluOpType
 FUNC = mybir.ActivationFunctionType
@@ -23,26 +26,24 @@ def tile_biojepa_kernel(tc, table, act, lnw, lnb, w1, b1, w2, b2, offs, out):
         nc.sync.dma_start(table_rows[:], table.rearrange("(b p) d -> p b d", p=P))
         act_rows = held.tile([P, D], F32)
         nc.scalar.dma_start(act_rows[:], act.rearrange("d o -> (d o)").partition_broadcast(P))
-        b1_cols = held.tile([P, HIDDEN_BLOCKS], F32)
-        with nc.allow_non_contiguous_dma(reason="512 biases, one to a partition and block"):
-            nc.scalar.dma_start(b1_cols[:], b1.rearrange("(k p) o -> p (k o)", p=P))
-        lnw_rows = held.tile([P, D], F32)
-        nc.sync.dma_start(lnw_rows[:], lnw.rearrange("d o -> (d o)").partition_broadcast(P))
-        lnb_rows = held.tile([P, D], F32)
-        nc.sync.dma_start(lnb_rows[:], lnb.rearrange("d o -> (d o)").partition_broadcast(P))
+        vector_rows = held.tile([P, P], F32)
+        nc.vector.memset(vector_rows[:], 0.0)
+        nc.sync.dma_start(vector_rows[B1 : B1 + HIDDEN_BLOCKS, :], b1.rearrange("(k p) o -> k (p o)", p=P))
+        nc.sync.dma_start(vector_rows[LNW : LNW + 1, :], lnw.rearrange("d o -> o d"))
+        nc.sync.dma_start(vector_rows[LNB : LNB + 1, :], lnb.rearrange("d o -> o d"))
+        nc.sync.dma_start(vector_rows[ACT : ACT + 1, :], act.rearrange("d o -> o d"))
+        nc.sync.dma_start(vector_rows[B2 : B2 + 1, :], b2.rearrange("d o -> o d"))
         offsets = held.tile([P, N // 16], U16)
         nc.sync.dma_start(offsets[:], offs)
         w1_sb = held.tile([P, F], BF16)
         nc.sync.dma_start(w1_sb[:], w1)
         w2_sb = held.tile([P, HIDDEN_BLOCKS, D], BF16)
         nc.sync.dma_start(w2_sb[:], w2.rearrange("(k p) d -> p k d", p=P))
-        act_col = held.tile([P, 1], F32)
-        nc.sync.dma_start(act_col[:], act)
-        b2_col = held.tile([P, 1], F32)
-        nc.sync.dma_start(b2_col[:], b2)
 
         identity_bf16 = held.tile([P, P], BF16)
         make_identity(nc, identity_bf16[:])
+        identity_f32 = held.tile([P, P], F32)
+        make_identity(nc, identity_f32[:])
         eps_col = held.tile([P, 1], F32)
         nc.vector.memset(eps_col[:], EPS)
 
@@ -50,6 +51,9 @@ def tile_biojepa_kernel(tc, table, act, lnw, lnb, w1, b1, w2, b2, offs, out):
         for b in range(WORD_BLOCKS):
             nc.tensor.transpose(table_flipped[:, b * P : (b + 1) * P], table_rows[:, b, :], identity_bf16[:])
         table_window = held.tile([P, S], BF16)
+        vector_flipped = psum.tile([P, P], F32, tag="hidden_psum3")
+        nc.tensor.transpose(vector_flipped[:], vector_rows[:], identity_f32[:])
+        vector_cols = held.tile([P, SMALL_VECTORS], F32)
 
         x = held.tile([P, WORD_BLOCKS, D], F32)
         stats = held.tile([P, WORD_BLOCKS, 6], F32)
@@ -62,26 +66,29 @@ def tile_biojepa_kernel(tc, table, act, lnw, lnb, w1, b1, w2, b2, offs, out):
             nc.vector.bn_aggr(mean_var[:, b, :], stats[:, b, :])
         std = held.tile([P, WORD_BLOCKS], F32)
         nc.scalar.activation(std[:], mean_var[:, :, 1], FUNC.Sqrt, bias=eps_col[:], scale=1.0)
-        centred = held.tile([P, WORD_BLOCKS, D], F32)
-        for b in range(WORD_BLOCKS):
-            nc.vector.scalar_tensor_tensor(
-                centred[:, b, :], x[:, b, :], mean_var[:, b, 0:1], lnw_rows[:], ALU.subtract, ALU.mult
-            )
+        nc.vector.tensor_copy(vector_cols[:], vector_flipped[:, 0:SMALL_VECTORS])
+        nc.vector.tensor_copy(table_window[:], table_flipped[:])
         rstd = held.tile([P, WORD_BLOCKS], F32)
         nc.vector.reciprocal(rstd[:], std[:])
-        n_rows = held.tile([P, WORD_BLOCKS, D], BF16)
+        z = held.tile([P, WORD_BLOCKS, D], F32)
         for b in range(WORD_BLOCKS):
-            nc.vector.scalar_tensor_tensor(
-                n_rows[:, b, :], centred[:, b, :], rstd[:, b : b + 1], lnb_rows[:], ALU.mult, ALU.add
+            nc.vector.tensor_scalar(
+                z[:, b, :], x[:, b, :], mean_var[:, b, 0:1], rstd[:, b : b + 1], ALU.subtract, ALU.mult
             )
 
-        n_flipped = [psum.tile([P, P], BF16, name=f"n_flipped{b}") for b in range(WORD_BLOCKS)]
-        for b in range(WORD_BLOCKS):
-            nc.tensor.transpose(n_flipped[b][:], n_rows[:, b, :], identity_bf16[:])
-        nc.vector.tensor_copy(table_window[:], table_flipped[:])
         n_window = held.tile([P, S], BF16)
+        z_flipped = [psum.tile([P, P], F32, name=f"z_flipped{b}") for b in range(WORD_BLOCKS)]
         for b in range(WORD_BLOCKS):
-            nc.vector.tensor_copy(n_window[:, b * P : (b + 1) * P], n_flipped[b][:])
+            nc.tensor.transpose(z_flipped[b][:], z[:, b, :], identity_f32[:])
+        for b in range(WORD_BLOCKS):
+            nc.vector.tensor_scalar(
+                n_window[:, b * P : (b + 1) * P],
+                z_flipped[b][:],
+                vector_cols[:, LNW : LNW + 1],
+                vector_cols[:, LNB : LNB + 1],
+                ALU.mult,
+                ALU.add,
+            )
 
         out_psum = psum.tile([P, N], F32)
         nc.tensor.matmul(
@@ -100,12 +107,18 @@ def tile_biojepa_kernel(tc, table, act, lnw, lnb, w1, b1, w2, b2, offs, out):
         h = held.tile([P, HIDDEN_BLOCKS, N], BF16)
         for k in range(HIDDEN_BLOCKS):
             nc.scalar.activation(
-                h[:, k, :], hidden_psum[k][:], FUNC.Gelu_apprx_tanh, bias=b1_cols[:, k : k + 1], scale=1.0
+                h[:, k, :],
+                hidden_psum[k][:],
+                FUNC.Gelu_apprx_tanh,
+                bias=vector_cols[:, B1 + k : B1 + k + 1],
+                scale=1.0,
             )
             nc.tensor.matmul(
                 out_psum[:], w2_sb[:, k, :], h[:, k, :], start=False, stop=(k == HIDDEN_BLOCKS - 1)
             )
 
         out_sb = held.tile([P, N], F32)
-        nc.vector.tensor_scalar(out_sb[:], out_psum[:], act_col[:], b2_col[:], ALU.add, ALU.add)
+        nc.vector.tensor_scalar(
+            out_sb[:], out_psum[:], vector_cols[:, ACT : ACT + 1], vector_cols[:, B2 : B2 + 1], ALU.add, ALU.add
+        )
         nc.sync.dma_start(out, out_sb[:])

import concourse.mybir as mybir
from concourse.masks import make_identity

S, D, F, N = 256, 128, 512, 128
P = 128
EPS = 1e-5
WORD_BLOCKS = S // P
HIDDEN_BLOCKS = F // P
FLOPS = 2 * N * D * F * 2

LNW, LNB, ACT, B2, B1 = 0, 1, 2, 3, 4
SMALL_VECTORS = B1 + HIDDEN_BLOCKS

BF16, F32, U16 = mybir.dt.bfloat16, mybir.dt.float32, mybir.dt.uint16
ALU = mybir.AluOpType
FUNC = mybir.ActivationFunctionType


def tile_biojepa_kernel(tc, table, act, lnw, lnb, w1, b1, w2, b2, offs, out):
    nc = tc.nc
    with (
        tc.tile_pool(name="held", bufs=1) as held,
        tc.psum_pool(name="psum", bufs=1) as psum,
    ):
        table_rows = held.tile([P, WORD_BLOCKS, D], BF16)
        nc.sync.dma_start(table_rows[:], table.rearrange("(b p) d -> p b d", p=P))
        act_rows = held.tile([P, D], F32)
        nc.scalar.dma_start(act_rows[:], act.rearrange("d o -> (d o)").partition_broadcast(P))
        vector_rows = held.tile([P, P], F32)
        nc.vector.memset(vector_rows[:], 0.0)
        nc.sync.dma_start(vector_rows[B1 : B1 + HIDDEN_BLOCKS, :], b1.rearrange("(k p) o -> k (p o)", p=P))
        nc.sync.dma_start(vector_rows[LNW : LNW + 1, :], lnw.rearrange("d o -> o d"))
        nc.sync.dma_start(vector_rows[LNB : LNB + 1, :], lnb.rearrange("d o -> o d"))
        nc.sync.dma_start(vector_rows[ACT : ACT + 1, :], act.rearrange("d o -> o d"))
        nc.sync.dma_start(vector_rows[B2 : B2 + 1, :], b2.rearrange("d o -> o d"))
        offsets = held.tile([P, N // 16], U16)
        nc.sync.dma_start(offsets[:], offs)
        w1_sb = held.tile([P, F], BF16)
        nc.sync.dma_start(w1_sb[:], w1)
        w2_sb = held.tile([P, HIDDEN_BLOCKS, D], BF16)
        nc.sync.dma_start(w2_sb[:], w2.rearrange("(k p) d -> p k d", p=P))

        identity_bf16 = held.tile([P, P], BF16)
        make_identity(nc, identity_bf16[:])
        identity_f32 = held.tile([P, P], F32)
        make_identity(nc, identity_f32[:])
        eps_col = held.tile([P, 1], F32)
        nc.vector.memset(eps_col[:], EPS)

        table_flipped = psum.tile([P, S], BF16)
        for b in range(WORD_BLOCKS):
            nc.tensor.transpose(table_flipped[:, b * P : (b + 1) * P], table_rows[:, b, :], identity_bf16[:])
        table_window = held.tile([P, S], BF16)
        vector_flipped = psum.tile([P, P], F32, tag="hidden_psum3")
        nc.tensor.transpose(vector_flipped[:], vector_rows[:], identity_f32[:])
        vector_cols = held.tile([P, SMALL_VECTORS], F32)

        x = held.tile([P, WORD_BLOCKS, D], F32)
        stats = held.tile([P, WORD_BLOCKS, 6], F32)
        mean_var = held.tile([P, WORD_BLOCKS, 2], F32)
        for b in range(WORD_BLOCKS):
            nc.vector.tensor_tensor(x[:, b, :], table_rows[:, b, :], act_rows[:], ALU.add)
        for b in range(WORD_BLOCKS):
            nc.vector.bn_stats(stats[:, b, :], x[:, b, :])
        for b in range(WORD_BLOCKS):
            nc.vector.bn_aggr(mean_var[:, b, :], stats[:, b, :])
        std = held.tile([P, WORD_BLOCKS], F32)
        nc.scalar.activation(std[:], mean_var[:, :, 1], FUNC.Sqrt, bias=eps_col[:], scale=1.0)
        nc.vector.tensor_copy(vector_cols[:], vector_flipped[:, 0:SMALL_VECTORS])
        nc.vector.tensor_copy(table_window[:], table_flipped[:])
        rstd = held.tile([P, WORD_BLOCKS], F32)
        nc.vector.reciprocal(rstd[:], std[:])
        z = held.tile([P, WORD_BLOCKS, D], F32)
        for b in range(WORD_BLOCKS):
            nc.vector.tensor_scalar(
                z[:, b, :], x[:, b, :], mean_var[:, b, 0:1], rstd[:, b : b + 1], ALU.subtract, ALU.mult
            )

        n_window = held.tile([P, S], BF16)
        z_flipped = [psum.tile([P, P], F32, name=f"z_flipped{b}") for b in range(WORD_BLOCKS)]
        for b in range(WORD_BLOCKS):
            nc.tensor.transpose(z_flipped[b][:], z[:, b, :], identity_f32[:])
        for b in range(WORD_BLOCKS):
            nc.vector.tensor_scalar(
                n_window[:, b * P : (b + 1) * P],
                z_flipped[b][:],
                vector_cols[:, LNW : LNW + 1],
                vector_cols[:, LNB : LNB + 1],
                ALU.mult,
                ALU.add,
            )

        out_psum = psum.tile([P, N], F32)
        nc.tensor.matmul(
            out_psum[:], identity_bf16[:], table_window[:].indirect(offsets[:]), start=True, stop=False
        )
        hidden_psum = [psum.tile([P, N], F32, name=f"hidden_psum{k}") for k in range(HIDDEN_BLOCKS)]
        for k in range(HIDDEN_BLOCKS):
            nc.tensor.matmul(
                hidden_psum[k][:],
                w1_sb[:, k * P : (k + 1) * P],
                n_window[:].indirect(offsets[:]),
                start=True,
                stop=True,
            )

        h = held.tile([P, HIDDEN_BLOCKS, N], BF16)
        for k in range(HIDDEN_BLOCKS):
            nc.scalar.activation(
                h[:, k, :],
                hidden_psum[k][:],
                FUNC.Gelu_apprx_tanh,
                bias=vector_cols[:, B1 + k : B1 + k + 1],
                scale=1.0,
            )
            nc.tensor.matmul(
                out_psum[:], w2_sb[:, k, :], h[:, k, :], start=False, stop=(k == HIDDEN_BLOCKS - 1)
            )

        out_sb = held.tile([P, N], F32)
        nc.vector.tensor_scalar(
            out_sb[:], out_psum[:], vector_cols[:, ACT : ACT + 1], vector_cols[:, B2 : B2 + 1], ALU.add, ALU.add
        )
        nc.sync.dma_start(out, out_sb[:])
